import numpy as np
import ml_dtypes


def mxq(x, axis, fmt="e4m3"):
    dtype, down = {"e4m3": (ml_dtypes.float8_e4m3fn, 7), "e5m2": (ml_dtypes.float8_e5m2, 14)}[fmt]
    v = np.moveaxis(np.asarray(x, np.float32).astype(ml_dtypes.bfloat16).astype(np.float64), axis, -1)
    blocks = v.reshape(v.shape[:-1] + (-1, 32))
    amax = np.abs(blocks).max(-1, keepdims=True)
    byte = np.maximum(np.where(amax > 0, np.frexp(amax)[1] - 1 + 127, 0) - down, 1)
    scale = np.exp2(byte - 127.0)
    codes = (blocks / scale).astype(np.float32).astype(dtype).astype(np.float64)
    return np.moveaxis((codes * scale).reshape(v.shape), -1, axis)


WIDE = False


def mx_kscale(k):
    if not WIDE:
        return np.ones(k)
    levels = np.array([10, -10, 5, -5, 0])
    a = np.random.permutation(np.resize(levels, k // 512 * 4)).reshape(k // 512, 4)
    idx = np.arange(k)
    return np.exp2(a[idx // 512, idx % 128 // 32])


BF16 = ml_dtypes.bfloat16


def bf(x):
    return np.asarray(x, np.float32).astype(BF16)


def f64(x):
    return np.asarray(x).astype(np.float64)


G, S, M, H, E, C = 2, 512, 512, 1024, 16, 64


def setup_inputs():
    s, t = mx_kscale(S), mx_kscale(M)
    return {"dispatch_mask": bf(np.random.standard_normal((G, S, E, C)) * 0.1 * s[None, :, None, None]),
            "x": bf(np.random.standard_normal((G, S, M)) / s[None, :, None] * t),
            "wi": bf(np.random.standard_normal((E, M, H)) * 10.0 / np.sqrt(S * M) / t[None, :, None])}


def reference(dispatch_mask, x, wi):
    dm = mxq(f64(dispatch_mask).reshape(G, S, E * C), 1, "e4m3")
    xq = mxq(f64(x), 1, "e4m3")
    d = dm.transpose(0, 2, 1) @ xq
    dispatched = d.reshape(G, E, C, M).transpose(1, 0, 2, 3)
    pre = mxq(dispatched.reshape(E, G * C, M), 2, "e4m3") @ mxq(f64(wi), 1, "e4m3")
    return np.maximum(pre, 0.0).reshape(E, G, C, H)

@@ -1,0 +1,200 @@
+from contextlib import ExitStack
+
+import concourse.mybir as mybir
+
+BF16 = mybir.dt.bfloat16
+F32 = mybir.dt.float32
+U32 = mybir.dt.uint32
+U8 = mybir.dt.uint8
+FP8X4 = mybir.dt.float8_e4m3fn_x4
+RELU = mybir.ActivationFunctionType.Relu
+
+G, S, M, H, E, C = 2, 512, 512, 1024, 16, 64
+P = 128
+PACK = 4
+SLOTS = E * C
+BANK = 512
+PAIR = 2
+RUN = 4
+
+VECTOR_COLUMNS = 736
+VECTOR_SLICES = 3
+
+RAW_BUFS = 8
+
+FLOPS = 2 * G * SLOTS * S * M + 2 * E * G * C * M * H
+
+
+def tile_flaxpositionwisemoelayer_pa_kernel(tc, dispatch_mask, x, wi, out):
+    nc = tc.nc
+    with ExitStack() as ctx:
+        keep = ctx.enter_context(tc.tile_pool(name="keep", bufs=1))
+        x_pool = ctx.enter_context(tc.tile_pool(name="x_pool", bufs=G))
+        raw_pool = ctx.enter_context(tc.tile_pool(name="raw_pool", bufs=RAW_BUFS))
+        grouped_pool = ctx.enter_context(tc.tile_pool(name="grouped_pool", bufs=3))
+        w_pool = ctx.enter_context(tc.tile_pool(name="w_pool", bufs=3))
+        d_pool = ctx.enter_context(tc.tile_pool(name="d_pool", bufs=3))
+        result_pool = ctx.enter_context(tc.tile_pool(name="result_pool", bufs=E))
+        d_psum = ctx.enter_context(tc.psum_pool(name="d_psum", bufs=3))
+        h_psum = ctx.enter_context(tc.psum_pool(name="h_psum", bufs=4))
+        ctx.enter_context(tc.manual_schedule())
+
+        wide_rows = [dispatch_mask[g].rearrange("s e c -> s (e c)") for g in range(G)] + [
+            wi[e] for e in range(E)
+        ]
+
+        x_raw, x_grouped, x_codes, x_scales = {}, {}, {}, {}
+        raw, grouped, codes, scales = {}, {}, {}, {}
+        d_grouped, d_codes, d_scales = {}, {}, {}
+        pre, result = {}, {}
+
+        def load_x(g):
+            x_raw[g] = x_pool.tile([P, PACK, M], BF16, name="x_raw", tag="x_raw")
+            nc.sync.dma_start(out=x_raw[g][:], in_=x[g].rearrange("(p j) m -> p j m", j=PACK))
+
+        def load_wide(k):
+            raw[k] = raw_pool.tile([P, PACK, H], BF16, name="raw", tag="raw")
+            nc.sync.dma_start(
+                out=raw[k][:], in_=wide_rows[k].rearrange("(p j) w -> p j w", j=PACK)
+            )
+
+        def regroup_x(g):
+            x_grouped[g] = x_pool.tile(
+                [P, M, PACK], BF16, name="x_grouped", tag="x_grouped", align_bytes=64
+            )
+            dst = x_grouped[g][:].rearrange("p (t q) j -> p t q j", t=PACK)
+            src = x_raw[g][:].rearrange("p j (q t) -> p t q j", t=PACK)
+            nc.vector.tensor_copy(out=dst[:, :VECTOR_SLICES], in_=src[:, :VECTOR_SLICES])
+            nc.scalar.copy(out=dst[:, VECTOR_SLICES:], in_=src[:, VECTOR_SLICES:])
+
+        def quantise_x(g):
+            x_codes[g] = keep.tile([P, M], U32, name="x_codes%d" % g, align_bytes=64)
+            x_scales[g] = keep.tile([P, M], U8, name="x_scales%d" % g, align_bytes=64)
+            nc.vector.quantize_mx(
+                out=x_codes[g][:].bitcast(FP8X4),
+                scales=x_scales[g][:],
+                in_=x_grouped[g][:].rearrange("p w j -> p (w j)"),
+            )
+
+        def regroup_wide(k):
+            grouped[k] = grouped_pool.tile(
+                [P, H, PACK], BF16, name="grouped", tag="grouped", align_bytes=64
+            )
+            dst = grouped[k][:].rearrange("p (r i) j -> p r j i", i=RUN)
+            src = raw[k][:].rearrange("p j (r i) -> p r j i", i=RUN)
+            border = VECTOR_COLUMNS // RUN
+            nc.vector.tensor_copy(out=dst[:, :border], in_=src[:, :border])
+            nc.scalar.copy(out=dst[:, border:], in_=src[:, border:])
+
+        def quantise_wide(k):
+            if k < G:
+                codes[k] = keep.tile([P, H], U32, name="mask_codes%d" % k, align_bytes=64)
+                scales[k] = keep.tile([P, H], U8, name="mask_scales%d" % k, align_bytes=64)
+            else:
+                codes[k] = w_pool.tile([P, H], U32, name="w_codes", tag="w_codes", align_bytes=64)
+                scales[k] = w_pool.tile([P, H], U8, name="w_scales", tag="w_scales", align_bytes=64)
+            nc.vector.quantize_mx(
+                out=codes[k][:].bitcast(FP8X4),
+                scales=scales[k][:],
+                in_=grouped[k][:].rearrange("p w j -> p (w j)"),
+            )
+
+        def dispatch(pair, g):
+            bank = d_psum.tile([P, PACK, PAIR * C], F32, name="d_bank", tag="d_bank")
+            slots = slice(pair * PAIR * C, (pair + 1) * PAIR * C)
+            for t in range(PACK):
+                m_slice = slice(t * P, (t + 1) * P)
+                nc.tensor.matmul_mx(
+                    out=bank[:, t, :],
+                    lhsT=x_codes[g][:, m_slice].bitcast(FP8X4),
+                    lhsT_scale=x_scales[g][:, m_slice],
+                    rhs=codes[g][:, slots].bitcast(FP8X4),
+                    rhs_scale=scales[g][:, slots],
+                    start=True,
+                    stop=True,
+                )
+            if g == 0:
+                d_grouped[pair] = d_pool.tile(
+                    [P, PAIR, G, C, PACK], BF16, name="d_grouped", tag="d_grouped", align_bytes=64
+                )
+            nc.scalar.copy(
+                out=d_grouped[pair][:, :, g, :, :],
+                in_=bank[:].rearrange("p t (e c) -> p e c t", e=PAIR),
+            )
+
+        def quantise_dispatched(pair):
+            d_codes[pair] = d_pool.tile(
+                [P, PAIR * G * C], U32, name="d_codes", tag="d_codes", align_bytes=64
+            )
+            d_scales[pair] = d_pool.tile(
+                [P, PAIR * G * C], U8, name="d_scales", tag="d_scales", align_bytes=64
+            )
+            nc.vector.quantize_mx(
+                out=d_codes[pair][:].bitcast(FP8X4),
+                scales=d_scales[pair][:],
+                in_=d_grouped[pair][:].rearrange("p e g c t -> p (e g c t)"),
+            )
+
+        def project(e):
+            pair = e // PAIR
+            rows = slice((e % PAIR) * G * C, (e % PAIR + 1) * G * C)
+            for half in range(H // BANK):
+                h_cols = slice(half * BANK, (half + 1) * BANK)
+                pre[e, half] = h_psum.tile([P, BANK], F32, name="pre", tag="pre")
+                nc.tensor.matmul_mx(
+                    out=pre[e, half][:],
+                    lhsT=d_codes[pair][:, rows].bitcast(FP8X4),
+                    lhsT_scale=d_scales[pair][:, rows],
+                    rhs=codes[G + e][:, h_cols].bitcast(FP8X4),
+                    rhs_scale=scales[G + e][:, h_cols],
+                    start=True,
+                    stop=True,
+                )
+
+        def relu(e):
+            result[e] = result_pool.tile([P, H], F32, name="result", tag="result")
+            for half in range(H // BANK):
+                h_cols = slice(half * BANK, (half + 1) * BANK)
+                nc.scalar.activation(out=result[e][:, h_cols], in_=pre[e, half][:], func=RELU)
+
+        for g in range(G):
+            load_x(g)
+        for k in range(RAW_BUFS):
+            load_wide(k)
+
+        def regroup_wide_and_refill(k):
+            regroup_wide(k)
+            if k + RAW_BUFS < G + E:
+                load_wide(k + RAW_BUFS)
+
+        warm = keep.tile([P, 1], F32, name="warm")
+        nc.vector.memset(warm[:], 0.0)
+        nc.scalar.activation(out=warm[:], in_=warm[:], func=RELU)
+
+        regroup_x(0)
+        regroup_x(1)
+        quantise_x(0)
+        regroup_wide_and_refill(0)
+        quantise_x(1)
+        regroup_wide_and_refill(1)
+        quantise_wide(0)
+        regroup_wide_and_refill(G)
+        quantise_wide(1)
+        for g in range(G):
+            dispatch(0, g)
+
+        for e in range(E):
+            if e + 1 < E:
+                regroup_wide_and_refill(G + e + 1)
+            if e + PAIR < E:
+                dispatch(e // PAIR + 1, e % PAIR)
+            if e % PAIR == 0:
+                quantise_dispatched(e // PAIR)
+            quantise_wide(G + e)
+            project(e)
+            if e >= 1:
+                relu(e - 1)
+        relu(E - 1)
+
+        for e in range(E):
+            nc.sync.dma_start(out=out[e].rearrange("g c h -> (g c) h"), in_=result[e][:])

@@ -17,10 +17,11 @@ BANK = 512
 PAIR = 2
 RUN = 4
 
-VECTOR_COLUMNS = 736
+VECTOR_COLUMNS = 696
 VECTOR_SLICES = 3
 
 RAW_BUFS = 8
+AHEAD = 2
 
 FLOPS = 2 * G * SLOTS * S * M + 2 * E * G * C * M * H
 
@@ -31,8 +32,9 @@ def tile_flaxpositionwisemoelayer_pa_kernel(tc, dispatch_mask, x, wi, out):
         keep = ctx.enter_context(tc.tile_pool(name="keep", bufs=1))
         x_pool = ctx.enter_context(tc.tile_pool(name="x_pool", bufs=G))
         raw_pool = ctx.enter_context(tc.tile_pool(name="raw_pool", bufs=RAW_BUFS))
-        grouped_pool = ctx.enter_context(tc.tile_pool(name="grouped_pool", bufs=3))
+        grouped_pool = ctx.enter_context(tc.tile_pool(name="grouped_pool", bufs=AHEAD + 2))
         w_pool = ctx.enter_context(tc.tile_pool(name="w_pool", bufs=3))
+        d_grouped_pool = ctx.enter_context(tc.tile_pool(name="d_grouped_pool", bufs=E // PAIR))
         d_pool = ctx.enter_context(tc.tile_pool(name="d_pool", bufs=3))
         result_pool = ctx.enter_context(tc.tile_pool(name="result_pool", bufs=E))
         d_psum = ctx.enter_context(tc.psum_pool(name="d_psum", bufs=3))
@@ -114,7 +116,7 @@ def tile_flaxpositionwisemoelayer_pa_kernel(tc, dispatch_mask, x, wi, out):
                     stop=True,
                 )
             if g == 0:
-                d_grouped[pair] = d_pool.tile(
+                d_grouped[pair] = d_grouped_pool.tile(
                     [P, PAIR, G, C, PACK], BF16, name="d_grouped", tag="d_grouped", align_bytes=64
                 )
             nc.scalar.copy(
@@ -155,11 +157,17 @@ def tile_flaxpositionwisemoelayer_pa_kernel(tc, dispatch_mask, x, wi, out):
             result[e] = result_pool.tile([P, H], F32, name="result", tag="result")
             for half in range(H // BANK):
                 h_cols = slice(half * BANK, (half + 1) * BANK)
-                nc.scalar.activation(out=result[e][:, h_cols], in_=pre[e, half][:], func=RELU)
+                if e < E - 1:
+                    nc.scalar.activation(out=result[e][:, h_cols], in_=pre[e, half][:], func=RELU)
+                else:
+                    nc.vector.tensor_scalar_max(
+                        out=result[e][:, h_cols], in0=pre[e, half][:], scalar1=0.0
+                    )
 
         for g in range(G):
             load_x(g)
-        for k in range(RAW_BUFS):
+            load_wide(g)
+        for k in range(G, RAW_BUFS):
             load_wide(k)
 
         def regroup_wide_and_refill(k):
@@ -172,23 +180,25 @@ def tile_flaxpositionwisemoelayer_pa_kernel(tc, dispatch_mask, x, wi, out):
         nc.scalar.activation(out=warm[:], in_=warm[:], func=RELU)
 
         regroup_x(0)
-        regroup_x(1)
         quantise_x(0)
         regroup_wide_and_refill(0)
-        quantise_x(1)
-        regroup_wide_and_refill(1)
+        regroup_x(1)
         quantise_wide(0)
+        regroup_wide_and_refill(1)
+        quantise_x(1)
+        for pair in range(E // PAIR):
+            dispatch(pair, 0)
         regroup_wide_and_refill(G)
         quantise_wide(1)
-        for g in range(G):
-            dispatch(0, g)
+        dispatch(0, 1)
+        regroup_wide_and_refill(G + 1)
 
         for e in range(E):
-            if e + 1 < E:
-                regroup_wide_and_refill(G + e + 1)
-            if e + PAIR < E:
-                dispatch(e // PAIR + 1, e % PAIR)
+            if e + AHEAD < E:
+                regroup_wide_and_refill(G + e + AHEAD)
             if e % PAIR == 0:
+                if e + PAIR < E:
+                    dispatch(e // PAIR + 1, 1)
                 quantise_dispatched(e // PAIR)
             quantise_wide(G + e)
             project(e)

@@ -1,5 +1,6 @@
 from contextlib import ExitStack
 
+import concourse.masks as masks
 import concourse.mybir as mybir
 
 BF16 = mybir.dt.bfloat16
@@ -20,6 +21,8 @@ RUN = 4
 VECTOR_COLUMNS = 696
 VECTOR_SLICES = 3
 
+PASS_COLUMNS = 128
+
 RAW_BUFS = 8
 AHEAD = 2
 
@@ -39,6 +42,7 @@ def tile_flaxpositionwisemoelayer_pa_kernel(tc, dispatch_mask, x, wi, out):
         result_pool = ctx.enter_context(tc.tile_pool(name="result_pool", bufs=E))
         d_psum = ctx.enter_context(tc.psum_pool(name="d_psum", bufs=3))
         h_psum = ctx.enter_context(tc.psum_pool(name="h_psum", bufs=4))
+        pass_psum = ctx.enter_context(tc.psum_pool(name="pass_psum", bufs=1))
         ctx.enter_context(tc.manual_schedule())
 
         wide_rows = [dispatch_mask[g].rearrange("s e c -> s (e c)") for g in range(G)] + [
@@ -49,6 +53,10 @@ def tile_flaxpositionwisemoelayer_pa_kernel(tc, dispatch_mask, x, wi, out):
         raw, grouped, codes, scales = {}, {}, {}, {}
         d_grouped, d_codes, d_scales = {}, {}, {}
         pre, result = {}, {}
+        passed = {}
+
+        identity = keep.tile([P, P], BF16, name="identity")
+        masks.make_identity(nc, identity[:])
 
         def load_x(g):
             x_raw[g] = x_pool.tile([P, PACK, M], BF16, name="x_raw", tag="x_raw")
@@ -78,6 +86,16 @@ def tile_flaxpositionwisemoelayer_pa_kernel(tc, dispatch_mask, x, wi, out):
                 in_=x_grouped[g][:].rearrange("p w j -> p (w j)"),
             )
 
+        def pass_through(k):
+            passed[k] = pass_psum.tile([P, PASS_COLUMNS, PACK], BF16, name="passed", tag="passed")
+            nc.tensor.matmul(
+                out=passed[k][:],
+                lhsT=identity[:],
+                rhs=raw[k][:, :, H - PASS_COLUMNS :].rearrange("p j c -> p c j"),
+                start=True,
+                stop=True,
+            )
+
         def regroup_wide(k):
             grouped[k] = grouped_pool.tile(
                 [P, H, PACK], BF16, name="grouped", tag="grouped", align_bytes=64
@@ -86,7 +104,12 @@ def tile_flaxpositionwisemoelayer_pa_kernel(tc, dispatch_mask, x, wi, out):
             src = raw[k][:].rearrange("p j (r i) -> p r j i", i=RUN)
             border = VECTOR_COLUMNS // RUN
             nc.vector.tensor_copy(out=dst[:, :border], in_=src[:, :border])
-            nc.scalar.copy(out=dst[:, border:], in_=src[:, border:])
+            end = (H - PASS_COLUMNS) // RUN
+            nc.scalar.copy(out=dst[:, border:end], in_=src[:, border:end])
+            nc.scalar.copy(
+                out=grouped[k][:, H - PASS_COLUMNS :, :].rearrange("p c j -> p (c j)"),
+                in_=passed[k][:].rearrange("p c j -> p (c j)"),
+            )
 
         def quantise_wide(k):
             if k < G:
@@ -179,19 +202,24 @@ def tile_flaxpositionwisemoelayer_pa_kernel(tc, dispatch_mask, x, wi, out):
         nc.vector.memset(warm[:], 0.0)
         nc.scalar.activation(out=warm[:], in_=warm[:], func=RELU)
 
+        pass_through(0)
         regroup_x(0)
         quantise_x(0)
         regroup_wide_and_refill(0)
+        pass_through(1)
         regroup_x(1)
         quantise_wide(0)
         regroup_wide_and_refill(1)
         quantise_x(1)
         for pair in range(E // PAIR):
             dispatch(pair, 0)
+        pass_through(G)
         regroup_wide_and_refill(G)
         quantise_wide(1)
         dispatch(0, 1)
+        pass_through(G + 1)
         regroup_wide_and_refill(G + 1)
+        pass_through(G + AHEAD)
 
         for e in range(E):
             if e + AHEAD < E:
@@ -202,6 +230,8 @@ def tile_flaxpositionwisemoelayer_pa_kernel(tc, dispatch_mask, x, wi, out):
                 quantise_dispatched(e // PAIR)
             quantise_wide(G + e)
             project(e)
+            if e + AHEAD + 1 < E:
+                pass_through(G + e + AHEAD + 1)
             if e >= 1:
                 relu(e - 1)
         relu(E - 1)

@@ -18,7 +18,7 @@ BANK = 512
 PAIR = 2
 RUN = 4
 
-VECTOR_COLUMNS = 696
+VECTOR_COLUMNS = 640
 VECTOR_SLICES = 3
 
 PASS_COLUMNS = 128

@@ -111,18 +111,22 @@ def tile_flaxpositionwisemoelayer_pa_kernel(tc, dispatch_mask, x, wi, out):
                 in_=passed[k][:].rearrange("p c j -> p (c j)"),
             )
 
-        def quantise_wide(k):
+        def quantise_wide(k, pieces=1, after_piece=None):
             if k < G:
                 codes[k] = keep.tile([P, H], U32, name="mask_codes%d" % k, align_bytes=64)
                 scales[k] = keep.tile([P, H], U8, name="mask_scales%d" % k, align_bytes=64)
             else:
                 codes[k] = w_pool.tile([P, H], U32, name="w_codes", tag="w_codes", align_bytes=64)
                 scales[k] = w_pool.tile([P, H], U8, name="w_scales", tag="w_scales", align_bytes=64)
-            nc.vector.quantize_mx(
-                out=codes[k][:].bitcast(FP8X4),
-                scales=scales[k][:],
-                in_=grouped[k][:].rearrange("p w j -> p (w j)"),
-            )
+            for first in range(0, H, H // pieces):
+                cols = slice(first, first + H // pieces)
+                nc.vector.quantize_mx(
+                    out=codes[k][:, cols].bitcast(FP8X4),
+                    scales=scales[k][:, cols],
+                    in_=grouped[k][:, cols, :].rearrange("p w j -> p (w j)"),
+                )
+                if after_piece is not None:
+                    after_piece(first)
 
         def dispatch(pair, g):
             bank = d_psum.tile([P, PACK, PAIR * C], F32, name="d_bank", tag="d_bank")
@@ -160,32 +164,44 @@ def tile_flaxpositionwisemoelayer_pa_kernel(tc, dispatch_mask, x, wi, out):
                 in_=d_grouped[pair][:].rearrange("p e g c t -> p (e g c t)"),
             )
 
-        def project(e):
+        def project_columns(e, first, width):
             pair = e // PAIR
             rows = slice((e % PAIR) * G * C, (e % PAIR + 1) * G * C)
-            for half in range(H // BANK):
-                h_cols = slice(half * BANK, (half + 1) * BANK)
-                pre[e, half] = h_psum.tile([P, BANK], F32, name="pre", tag="pre")
-                nc.tensor.matmul_mx(
-                    out=pre[e, half][:],
-                    lhsT=d_codes[pair][:, rows].bitcast(FP8X4),
-                    lhsT_scale=d_scales[pair][:, rows],
-                    rhs=codes[G + e][:, h_cols].bitcast(FP8X4),
-                    rhs_scale=scales[G + e][:, h_cols],
-                    start=True,
-                    stop=True,
+            h_cols = slice(first, first + width)
+            pre[e, first] = h_psum.tile([P, width], F32, name="pre", tag="pre")
+            nc.tensor.matmul_mx(
+                out=pre[e, first][:],
+                lhsT=d_codes[pair][:, rows].bitcast(FP8X4),
+                lhsT_scale=d_scales[pair][:, rows],
+                rhs=codes[G + e][:, h_cols].bitcast(FP8X4),
+                rhs_scale=scales[G + e][:, h_cols],
+                start=True,
+                stop=True,
+            )
+
+        def project(e):
+            for first in range(0, H, BANK):
+                project_columns(e, first, BANK)
+
+        def relu_columns(e, first, width, on_vector=False):
+            h_cols = slice(first, first + width)
+            if on_vector:
+                nc.vector.tensor_scalar_max(
+                    out=result[e][:, h_cols], in0=pre[e, first][:], scalar1=0.0
                 )
+            else:
+                nc.scalar.activation(out=result[e][:, h_cols], in_=pre[e, first][:], func=RELU)
 
         def relu(e):
             result[e] = result_pool.tile([P, H], F32, name="result", tag="result")
-            for half in range(H // BANK):
-                h_cols = slice(half * BANK, (half + 1) * BANK)
-                if e < E - 1:
-                    nc.scalar.activation(out=result[e][:, h_cols], in_=pre[e, half][:], func=RELU)
-                else:
-                    nc.vector.tensor_scalar_max(
-                        out=result[e][:, h_cols], in0=pre[e, half][:], scalar1=0.0
-                    )
+            for first in range(0, H, BANK):
+                relu_columns(e, first, BANK)
+
+        def store_columns(e, first, width):
+            h_cols = slice(first, first + width)
+            nc.sync.dma_start(
+                out=out[e].rearrange("g c h -> (g c) h")[:, h_cols], in_=result[e][:, h_cols]
+            )
 
         for g in range(G):
             load_x(g)
@@ -221,7 +237,7 @@ def tile_flaxpositionwisemoelayer_pa_kernel(tc, dispatch_mask, x, wi, out):
         regroup_wide_and_refill(G + 1)
         pass_through(G + AHEAD)
 
-        for e in range(E):
+        for e in range(E - 1):
             if e + AHEAD < E:
                 regroup_wide_and_refill(G + e + AHEAD)
             if e % PAIR == 0:
@@ -234,7 +250,24 @@ def tile_flaxpositionwisemoelayer_pa_kernel(tc, dispatch_mask, x, wi, out):
                 pass_through(G + e + AHEAD + 1)
             if e >= 1:
                 relu(e - 1)
-        relu(E - 1)
 
-        for e in range(E):
-            nc.sync.dma_start(out=out[e].rearrange("g c h -> (g c) h"), in_=result[e][:])
+        last = E - 1
+        result[last] = result_pool.tile([P, H], F32, name="result", tag="result")
+
+        def project_piece(first):
+            if first == 0:
+                project_columns(last, 0, BANK)
+                relu(last - 1)
+            else:
+                project_columns(last, BANK, BANK // 2)
+                project_columns(last, BANK + BANK // 2, BANK // 2)
+
+        quantise_wide(G + last, pieces=H // BANK, after_piece=project_piece)
+        relu_columns(last, 0, BANK)
+        relu_columns(last, BANK, BANK // 2, on_vector=True)
+        relu_columns(last, BANK + BANK // 2, BANK // 2)
+
+        for e in range(E - 1):
+            store_columns(e, 0, H)
+        for first in range(0, H, BANK):
+            store_columns(last, first, BANK)

@@ -19,10 +19,10 @@ PAIR = 2
 RUN = 4
 
 VECTOR_COLUMNS = 640
+PASS_COLUMNS = 128
 VECTOR_SLICES = 3
 
-PASS_COLUMNS = 128
-
+HEAD_PIECES = 2
 RAW_BUFS = 8
 AHEAD = 2
 
@@ -33,6 +33,7 @@ def tile_flaxpositionwisemoelayer_pa_kernel(tc, dispatch_mask, x, wi, out):
     nc = tc.nc
     with ExitStack() as ctx:
         keep = ctx.enter_context(tc.tile_pool(name="keep", bufs=1))
+        x_raw_pool = ctx.enter_context(tc.tile_pool(name="x_raw_pool", bufs=HEAD_PIECES + 1))
         x_pool = ctx.enter_context(tc.tile_pool(name="x_pool", bufs=G))
         raw_pool = ctx.enter_context(tc.tile_pool(name="raw_pool", bufs=RAW_BUFS))
         grouped_pool = ctx.enter_context(tc.tile_pool(name="grouped_pool", bufs=AHEAD + 2))
@@ -45,9 +46,16 @@ def tile_flaxpositionwisemoelayer_pa_kernel(tc, dispatch_mask, x, wi, out):
         pass_psum = ctx.enter_context(tc.psum_pool(name="pass_psum", bufs=1))
         ctx.enter_context(tc.manual_schedule())
 
-        wide_rows = [dispatch_mask[g].rearrange("s e c -> s (e c)") for g in range(G)] + [
-            wi[e] for e in range(E)
-        ]
+        mask_rows = [dispatch_mask[g].rearrange("s e c -> s (e c)") for g in range(G)]
+        piece = SLOTS // HEAD_PIECES
+        unit_rows = (
+            [mask_rows[0][:, h * piece : (h + 1) * piece] for h in range(HEAD_PIECES)]
+            + [mask_rows[1]]
+            + [wi[e] for e in range(E)]
+        )
+        MASK1 = HEAD_PIECES
+        W0 = HEAD_PIECES + 1
+        UNITS = len(unit_rows)
 
         x_raw, x_grouped, x_codes, x_scales = {}, {}, {}, {}
         raw, grouped, codes, scales = {}, {}, {}, {}
@@ -58,24 +66,32 @@ def tile_flaxpositionwisemoelayer_pa_kernel(tc, dispatch_mask, x, wi, out):
         identity = keep.tile([P, P], BF16, name="identity")
         masks.make_identity(nc, identity[:])
 
-        def load_x(g):
-            x_raw[g] = x_pool.tile([P, PACK, M], BF16, name="x_raw", tag="x_raw")
-            nc.sync.dma_start(out=x_raw[g][:], in_=x[g].rearrange("(p j) m -> p j m", j=PACK))
+        def load_x(g, pieces):
+            width = M // pieces
+            for h in range(pieces):
+                x_raw[g, h] = x_raw_pool.tile([P, PACK, width], BF16, name="x_raw", tag="x_raw")
+                nc.sync.dma_start(
+                    out=x_raw[g, h][:],
+                    in_=x[g][:, h * width : (h + 1) * width].rearrange("(p j) m -> p j m", j=PACK),
+                )
 
-        def load_wide(k):
-            raw[k] = raw_pool.tile([P, PACK, H], BF16, name="raw", tag="raw")
-            nc.sync.dma_start(
-                out=raw[k][:], in_=wide_rows[k].rearrange("(p j) w -> p j w", j=PACK)
-            )
+        def load_unit(u):
+            width = unit_rows[u].shape[1]
+            raw[u] = raw_pool.tile([P, PACK, width], BF16, name="raw", tag="raw")
+            nc.sync.dma_start(out=raw[u][:], in_=unit_rows[u].rearrange("(p j) w -> p j w", j=PACK))
 
-        def regroup_x(g):
+        def regroup_x(g, pieces):
             x_grouped[g] = x_pool.tile(
                 [P, M, PACK], BF16, name="x_grouped", tag="x_grouped", align_bytes=64
             )
-            dst = x_grouped[g][:].rearrange("p (t q) j -> p t q j", t=PACK)
-            src = x_raw[g][:].rearrange("p j (q t) -> p t q j", t=PACK)
-            nc.vector.tensor_copy(out=dst[:, :VECTOR_SLICES], in_=src[:, :VECTOR_SLICES])
-            nc.scalar.copy(out=dst[:, VECTOR_SLICES:], in_=src[:, VECTOR_SLICES:])
+            q_count = P // pieces
+            for h in range(pieces):
+                dst = x_grouped[g][:].rearrange("p (t q) j -> p t q j", t=PACK)[
+                    :, :, h * q_count : (h + 1) * q_count, :
+                ]
+                src = x_raw[g, h][:].rearrange("p j (q t) -> p t q j", t=PACK)
+                nc.vector.tensor_copy(out=dst[:, :VECTOR_SLICES], in_=src[:, :VECTOR_SLICES])
+                nc.scalar.copy(out=dst[:, VECTOR_SLICES:], in_=src[:, VECTOR_SLICES:])
 
         def quantise_x(g):
             x_codes[g] = keep.tile([P, M], U32, name="x_codes%d" % g, align_bytes=64)
@@ -86,59 +102,70 @@ def tile_flaxpositionwisemoelayer_pa_kernel(tc, dispatch_mask, x, wi, out):
                 in_=x_grouped[g][:].rearrange("p w j -> p (w j)"),
             )
 
-        def pass_through(k):
-            passed[k] = pass_psum.tile([P, PASS_COLUMNS, PACK], BF16, name="passed", tag="passed")
+        def pass_through(u):
+            width = unit_rows[u].shape[1]
+            count = PASS_COLUMNS * width // H
+            passed[u] = pass_psum.tile([P, count, PACK], BF16, name="passed", tag="passed")
             nc.tensor.matmul(
-                out=passed[k][:],
+                out=passed[u][:],
                 lhsT=identity[:],
-                rhs=raw[k][:, :, H - PASS_COLUMNS :].rearrange("p j c -> p c j"),
+                rhs=raw[u][:, :, width - count :].rearrange("p j c -> p c j"),
                 start=True,
                 stop=True,
             )
 
-        def regroup_wide(k):
-            grouped[k] = grouped_pool.tile(
-                [P, H, PACK], BF16, name="grouped", tag="grouped", align_bytes=64
+        def regroup_unit(u):
+            width = unit_rows[u].shape[1]
+            count = PASS_COLUMNS * width // H
+            grouped[u] = grouped_pool.tile(
+                [P, width, PACK], BF16, name="grouped", tag="grouped", align_bytes=64
             )
-            dst = grouped[k][:].rearrange("p (r i) j -> p r j i", i=RUN)
-            src = raw[k][:].rearrange("p j (r i) -> p r j i", i=RUN)
-            border = VECTOR_COLUMNS // RUN
+            dst = grouped[u][:].rearrange("p (r i) j -> p r j i", i=RUN)
+            src = raw[u][:].rearrange("p j (r i) -> p r j i", i=RUN)
+            border = VECTOR_COLUMNS * width // H // RUN
+            end = (width - count) // RUN
             nc.vector.tensor_copy(out=dst[:, :border], in_=src[:, :border])
-            end = (H - PASS_COLUMNS) // RUN
             nc.scalar.copy(out=dst[:, border:end], in_=src[:, border:end])
             nc.scalar.copy(
-                out=grouped[k][:, H - PASS_COLUMNS :, :].rearrange("p c j -> p (c j)"),
-                in_=passed[k][:].rearrange("p c j -> p (c j)"),
+                out=grouped[u][:, width - count :, :].rearrange("p c j -> p (c j)"),
+                in_=passed[u][:].rearrange("p c j -> p (c j)"),
             )
+            if u + RAW_BUFS < UNITS:
+                load_unit(u + RAW_BUFS)
 
-        def quantise_wide(k, pieces=1, after_piece=None):
-            if k < G:
-                codes[k] = keep.tile([P, H], U32, name="mask_codes%d" % k, align_bytes=64)
-                scales[k] = keep.tile([P, H], U8, name="mask_scales%d" % k, align_bytes=64)
+        def quantise_unit(u, pieces=1, after_piece=None):
+            width = unit_rows[u].shape[1]
+            if u < W0:
+                codes[u] = keep.tile([P, width], U32, name="mask_codes%d" % u, align_bytes=64)
+                scales[u] = keep.tile([P, width], U8, name="mask_scales%d" % u, align_bytes=64)
             else:
-                codes[k] = w_pool.tile([P, H], U32, name="w_codes", tag="w_codes", align_bytes=64)
-                scales[k] = w_pool.tile([P, H], U8, name="w_scales", tag="w_scales", align_bytes=64)
-            for first in range(0, H, H // pieces):
-                cols = slice(first, first + H // pieces)
+                codes[u] = w_pool.tile([P, H], U32, name="w_codes", tag="w_codes", align_bytes=64)
+                scales[u] = w_pool.tile([P, H], U8, name="w_scales", tag="w_scales", align_bytes=64)
+            for first in range(0, width, width // pieces):
+                cols = slice(first, first + width // pieces)
                 nc.vector.quantize_mx(
-                    out=codes[k][:, cols].bitcast(FP8X4),
-                    scales=scales[k][:, cols],
-                    in_=grouped[k][:, cols, :].rearrange("p w j -> p (w j)"),
+                    out=codes[u][:, cols].bitcast(FP8X4),
+                    scales=scales[u][:, cols],
+                    in_=grouped[u][:, cols, :].rearrange("p w j -> p (w j)"),
                 )
                 if after_piece is not None:
                     after_piece(first)
 
         def dispatch(pair, g):
             bank = d_psum.tile([P, PACK, PAIR * C], F32, name="d_bank", tag="d_bank")
-            slots = slice(pair * PAIR * C, (pair + 1) * PAIR * C)
+            first = pair * PAIR * C
+            u = first // piece if g == 0 else MASK1
+            if g == 0:
+                first = first % piece
+            slots = slice(first, first + PAIR * C)
             for t in range(PACK):
                 m_slice = slice(t * P, (t + 1) * P)
                 nc.tensor.matmul_mx(
                     out=bank[:, t, :],
                     lhsT=x_codes[g][:, m_slice].bitcast(FP8X4),
                     lhsT_scale=x_scales[g][:, m_slice],
-                    rhs=codes[g][:, slots].bitcast(FP8X4),
-                    rhs_scale=scales[g][:, slots],
+                    rhs=codes[u][:, slots].bitcast(FP8X4),
+                    rhs_scale=scales[u][:, slots],
                     start=True,
                     stop=True,
                 )
@@ -173,8 +200,8 @@ def tile_flaxpositionwisemoelayer_pa_kernel(tc, dispatch_mask, x, wi, out):
                 out=pre[e, first][:],
                 lhsT=d_codes[pair][:, rows].bitcast(FP8X4),
                 lhsT_scale=d_scales[pair][:, rows],
-                rhs=codes[G + e][:, h_cols].bitcast(FP8X4),
-                rhs_scale=scales[G + e][:, h_cols],
+                rhs=codes[W0 + e][:, h_cols].bitcast(FP8X4),
+                rhs_scale=scales[W0 + e][:, h_cols],
                 start=True,
                 stop=True,
             )
@@ -203,51 +230,53 @@ def tile_flaxpositionwisemoelayer_pa_kernel(tc, dispatch_mask, x, wi, out):
                 out=out[e].rearrange("g c h -> (g c) h")[:, h_cols], in_=result[e][:, h_cols]
             )
 
-        for g in range(G):
-            load_x(g)
-            load_wide(g)
-        for k in range(G, RAW_BUFS):
-            load_wide(k)
-
-        def regroup_wide_and_refill(k):
-            regroup_wide(k)
-            if k + RAW_BUFS < G + E:
-                load_wide(k + RAW_BUFS)
+        load_x(0, HEAD_PIECES)
+        for u in range(MASK1):
+            load_unit(u)
+        load_x(1, 1)
+        for u in range(MASK1, RAW_BUFS):
+            load_unit(u)
 
         warm = keep.tile([P, 1], F32, name="warm")
         nc.vector.memset(warm[:], 0.0)
         nc.scalar.activation(out=warm[:], in_=warm[:], func=RELU)
 
+        pairs_a_piece = E // PAIR // HEAD_PIECES
         pass_through(0)
-        regroup_x(0)
-        quantise_x(0)
-        regroup_wide_and_refill(0)
+        regroup_x(0, HEAD_PIECES)
+        regroup_unit(0)
         pass_through(1)
-        regroup_x(1)
-        quantise_wide(0)
-        regroup_wide_and_refill(1)
-        quantise_x(1)
-        for pair in range(E // PAIR):
+        quantise_x(0)
+        regroup_unit(1)
+        quantise_unit(0)
+        for pair in range(pairs_a_piece):
             dispatch(pair, 0)
-        pass_through(G)
-        regroup_wide_and_refill(G)
-        quantise_wide(1)
+        regroup_x(1, 1)
+        quantise_unit(1)
+        pass_through(MASK1)
+        regroup_unit(MASK1)
+        quantise_x(1)
+        for pair in range(pairs_a_piece, E // PAIR):
+            dispatch(pair, 0)
+        pass_through(W0)
+        regroup_unit(W0)
+        quantise_unit(MASK1)
         dispatch(0, 1)
-        pass_through(G + 1)
-        regroup_wide_and_refill(G + 1)
-        pass_through(G + AHEAD)
+        pass_through(W0 + 1)
+        regroup_unit(W0 + 1)
+        pass_through(W0 + AHEAD)
 
         for e in range(E - 1):
             if e + AHEAD < E:
-                regroup_wide_and_refill(G + e + AHEAD)
+                regroup_unit(W0 + e + AHEAD)
             if e % PAIR == 0:
                 if e + PAIR < E:
                     dispatch(e // PAIR + 1, 1)
                 quantise_dispatched(e // PAIR)
-            quantise_wide(G + e)
+            quantise_unit(W0 + e)
             project(e)
             if e + AHEAD + 1 < E:
-                pass_through(G + e + AHEAD + 1)
+                pass_through(W0 + e + AHEAD + 1)
             if e >= 1:
                 relu(e - 1)
 
@@ -262,7 +291,7 @@ def tile_flaxpositionwisemoelayer_pa_kernel(tc, dispatch_mask, x, wi, out):
                 project_columns(last, BANK, BANK // 2)
                 project_columns(last, BANK + BANK // 2, BANK // 2)
 
-        quantise_wide(G + last, pieces=H // BANK, after_piece=project_piece)
+        quantise_unit(W0 + last, pieces=H // BANK, after_piece=project_piece)
         relu_columns(last, 0, BANK)
         relu_columns(last, BANK, BANK // 2, on_vector=True)
         relu_columns(last, BANK + BANK // 2, BANK // 2)

@@ -41,8 +41,7 @@ def tile_flaxpositionwisemoelayer_pa_kernel(tc, dispatch_mask, x, wi, out):
         d_grouped_pool = ctx.enter_context(tc.tile_pool(name="d_grouped_pool", bufs=E // PAIR))
         d_pool = ctx.enter_context(tc.tile_pool(name="d_pool", bufs=3))
         result_pool = ctx.enter_context(tc.tile_pool(name="result_pool", bufs=E))
-        d_psum = ctx.enter_context(tc.psum_pool(name="d_psum", bufs=3))
-        h_psum = ctx.enter_context(tc.psum_pool(name="h_psum", bufs=4))
+        banks = ctx.enter_context(tc.psum_pool(name="banks", bufs=7))
         pass_psum = ctx.enter_context(tc.psum_pool(name="pass_psum", bufs=1))
         ctx.enter_context(tc.manual_schedule())
 
@@ -152,7 +151,7 @@ def tile_flaxpositionwisemoelayer_pa_kernel(tc, dispatch_mask, x, wi, out):
                     after_piece(first)
 
         def dispatch(pair, g):
-            bank = d_psum.tile([P, PACK, PAIR * C], F32, name="d_bank", tag="d_bank")
+            bank = banks.tile([P, PACK, PAIR * C], F32, name="bank", tag="bank")
             first = pair * PAIR * C
             u = first // piece if g == 0 else MASK1
             if g == 0:
@@ -195,7 +194,7 @@ def tile_flaxpositionwisemoelayer_pa_kernel(tc, dispatch_mask, x, wi, out):
             pair = e // PAIR
             rows = slice((e % PAIR) * G * C, (e % PAIR + 1) * G * C)
             h_cols = slice(first, first + width)
-            pre[e, first] = h_psum.tile([P, width], F32, name="pre", tag="pre")
+            pre[e, first] = banks.tile([P, width], F32, name="bank", tag="bank")
             nc.tensor.matmul_mx(
                 out=pre[e, first][:],
                 lhsT=d_codes[pair][:, rows].bitcast(FP8X4),
@@ -247,11 +246,11 @@ def tile_flaxpositionwisemoelayer_pa_kernel(tc, dispatch_mask, x, wi, out):
         regroup_unit(0)
         pass_through(1)
         quantise_x(0)
-        regroup_unit(1)
         quantise_unit(0)
+        regroup_unit(1)
+        regroup_x(1, 1)
         for pair in range(pairs_a_piece):
             dispatch(pair, 0)
-        regroup_x(1, 1)
         quantise_unit(1)
         pass_through(MASK1)
         regroup_unit(MASK1)

@@ -79,7 +79,9 @@ def tile_flaxpositionwisemoelayer_pa_kernel(tc, dispatch_mask, x, wi, out):
             raw[u] = raw_pool.tile([P, PACK, width], BF16, name="raw", tag="raw")
             nc.sync.dma_start(out=raw[u][:], in_=unit_rows[u].rearrange("(p j) w -> p j w", j=PACK))
 
-        def regroup_x(g, pieces):
+        def regroup_x(g, loaded_pieces):
+            pieces = HEAD_PIECES
+            width = M // pieces
             x_grouped[g] = x_pool.tile(
                 [P, M, PACK], BF16, name="x_grouped", tag="x_grouped", align_bytes=64
             )
@@ -88,7 +90,11 @@ def tile_flaxpositionwisemoelayer_pa_kernel(tc, dispatch_mask, x, wi, out):
                 dst = x_grouped[g][:].rearrange("p (t q) j -> p t q j", t=PACK)[
                     :, :, h * q_count : (h + 1) * q_count, :
                 ]
-                src = x_raw[g, h][:].rearrange("p j (q t) -> p t q j", t=PACK)
+                if loaded_pieces == pieces:
+                    columns = x_raw[g, h][:]
+                else:
+                    columns = x_raw[g, 0][:, :, h * width : (h + 1) * width]
+                src = columns.rearrange("p j (q t) -> p t q j", t=PACK)
                 nc.vector.tensor_copy(out=dst[:, :VECTOR_SLICES], in_=src[:, :VECTOR_SLICES])
                 nc.scalar.copy(out=dst[:, VECTOR_SLICES:], in_=src[:, VECTOR_SLICES:])
 

@@ -16,7 +16,7 @@ PACK = 4
 SLOTS = E * C
 BANK = 512
 PAIR = 2
-RUN = 4
+RUN = 8
 
 VECTOR_COLUMNS = 640
 PASS_COLUMNS = 128

@@ -18,9 +18,10 @@ BANK = 512
 PAIR = 2
 RUN = 8
 
-VECTOR_COLUMNS = 640
-PASS_COLUMNS = 128
-VECTOR_SLICES = 3
+MASK_VECTOR_COLUMNS = 640
+EVEN_VECTOR_COLUMNS = 512
+PASS_COLUMNS = 256
+PASS_STEP = 128
 
 HEAD_PIECES = 2
 RAW_BUFS = 8
@@ -95,8 +96,7 @@ def tile_flaxpositionwisemoelayer_pa_kernel(tc, dispatch_mask, x, wi, out):
                 else:
                     columns = x_raw[g, 0][:, :, h * width : (h + 1) * width]
                 src = columns.rearrange("p j (q t) -> p t q j", t=PACK)
-                nc.vector.tensor_copy(out=dst[:, :VECTOR_SLICES], in_=src[:, :VECTOR_SLICES])
-                nc.scalar.copy(out=dst[:, VECTOR_SLICES:], in_=src[:, VECTOR_SLICES:])
+                nc.vector.tensor_copy(out=dst, in_=src)
 
         def quantise_x(g):
             x_codes[g] = keep.tile([P, M], U32, name="x_codes%d" % g, align_bytes=64)
@@ -107,34 +107,42 @@ def tile_flaxpositionwisemoelayer_pa_kernel(tc, dispatch_mask, x, wi, out):
                 in_=x_grouped[g][:].rearrange("p w j -> p (w j)"),
             )
 
+        def is_passed(u):
+            return u >= W0 and (u - W0) % 2 == 1
+
         def pass_through(u):
-            width = unit_rows[u].shape[1]
-            count = PASS_COLUMNS * width // H
-            passed[u] = pass_psum.tile([P, count, PACK], BF16, name="passed", tag="passed")
-            nc.tensor.matmul(
-                out=passed[u][:],
-                lhsT=identity[:],
-                rhs=raw[u][:, :, width - count :].rearrange("p j c -> p c j"),
-                start=True,
-                stop=True,
-            )
+            passed[u] = pass_psum.tile([P, PASS_COLUMNS, PACK], BF16, name="passed", tag="passed")
+            for first in range(0, PASS_COLUMNS, PASS_STEP):
+                start = H - PASS_COLUMNS + first
+                nc.tensor.matmul(
+                    out=passed[u][:, first : first + PASS_STEP, :],
+                    lhsT=identity[:],
+                    rhs=raw[u][:, :, start : start + PASS_STEP].rearrange("p j c -> p c j"),
+                    start=True,
+                    stop=True,
+                )
 
         def regroup_unit(u):
             width = unit_rows[u].shape[1]
-            count = PASS_COLUMNS * width // H
+            if is_passed(u):
+                border = width - PASS_COLUMNS
+            else:
+                share = MASK_VECTOR_COLUMNS if u < W0 else EVEN_VECTOR_COLUMNS
+                border = share * width // H
             grouped[u] = grouped_pool.tile(
                 [P, width, PACK], BF16, name="grouped", tag="grouped", align_bytes=64
             )
             dst = grouped[u][:].rearrange("p (r i) j -> p r j i", i=RUN)
             src = raw[u][:].rearrange("p j (r i) -> p r j i", i=RUN)
-            border = VECTOR_COLUMNS * width // H // RUN
-            end = (width - count) // RUN
-            nc.vector.tensor_copy(out=dst[:, :border], in_=src[:, :border])
-            nc.scalar.copy(out=dst[:, border:end], in_=src[:, border:end])
-            nc.scalar.copy(
-                out=grouped[u][:, width - count :, :].rearrange("p c j -> p (c j)"),
-                in_=passed[u][:].rearrange("p c j -> p (c j)"),
-            )
+            runs = border // RUN
+            nc.vector.tensor_copy(out=dst[:, :runs], in_=src[:, :runs])
+            if is_passed(u):
+                nc.scalar.copy(
+                    out=grouped[u][:, border:, :].rearrange("p c j -> p (c j)"),
+                    in_=passed[u][:].rearrange("p c j -> p (c j)"),
+                )
+            else:
+                nc.scalar.copy(out=dst[:, runs:], in_=src[:, runs:])
             if u + RAW_BUFS < UNITS:
                 load_unit(u + RAW_BUFS)
 
@@ -247,10 +255,8 @@ def tile_flaxpositionwisemoelayer_pa_kernel(tc, dispatch_mask, x, wi, out):
         nc.scalar.activation(out=warm[:], in_=warm[:], func=RELU)
 
         pairs_a_piece = E // PAIR // HEAD_PIECES
-        pass_through(0)
         regroup_x(0, HEAD_PIECES)
         regroup_unit(0)
-        pass_through(1)
         quantise_x(0)
         quantise_unit(0)
         regroup_unit(1)
@@ -258,18 +264,15 @@ def tile_flaxpositionwisemoelayer_pa_kernel(tc, dispatch_mask, x, wi, out):
         for pair in range(pairs_a_piece):
             dispatch(pair, 0)
         quantise_unit(1)
-        pass_through(MASK1)
         regroup_unit(MASK1)
         quantise_x(1)
         for pair in range(pairs_a_piece, E // PAIR):
             dispatch(pair, 0)
-        pass_through(W0)
         regroup_unit(W0)
         quantise_unit(MASK1)
         dispatch(0, 1)
         pass_through(W0 + 1)
         regroup_unit(W0 + 1)
-        pass_through(W0 + AHEAD)
 
         for e in range(E - 1):
             if e + AHEAD < E:
@@ -279,9 +282,9 @@ def tile_flaxpositionwisemoelayer_pa_kernel(tc, dispatch_mask, x, wi, out):
                     dispatch(e // PAIR + 1, 1)
                 quantise_dispatched(e // PAIR)
             quantise_unit(W0 + e)
-            project(e)
-            if e + AHEAD + 1 < E:
+            if e + AHEAD + 1 < E and is_passed(W0 + e + AHEAD + 1):
                 pass_through(W0 + e + AHEAD + 1)
+            project(e)
             if e >= 1:
                 relu(e - 1)
 

@@ -16,7 +16,7 @@ PACK = 4
 SLOTS = E * C
 BANK = 512
 PAIR = 2
-RUN = 8
+RUN = 2
 
 MASK_VECTOR_COLUMNS = 640
 EVEN_VECTOR_COLUMNS = 512

@@ -90,12 +90,12 @@ def tile_flaxpositionwisemoelayer_pa_kernel(tc, dispatch_mask, x, wi, out):
             for h in range(pieces):
                 dst = x_grouped[g][:].rearrange("p (t q) j -> p t q j", t=PACK)[
                     :, :, h * q_count : (h + 1) * q_count, :
-                ]
+                ].rearrange("p t (r i) j -> p t r j i", i=RUN)
                 if loaded_pieces == pieces:
                     columns = x_raw[g, h][:]
                 else:
                     columns = x_raw[g, 0][:, :, h * width : (h + 1) * width]
-                src = columns.rearrange("p j (q t) -> p t q j", t=PACK)
+                src = columns.rearrange("p j (r i t) -> p t r j i", i=RUN, t=PACK)
                 nc.vector.tensor_copy(out=dst, in_=src)
 
         def quantise_x(g):

from contextlib import ExitStack

import concourse.masks as masks
import concourse.mybir as mybir

BF16 = mybir.dt.bfloat16
F32 = mybir.dt.float32
U32 = mybir.dt.uint32
U8 = mybir.dt.uint8
FP8X4 = mybir.dt.float8_e4m3fn_x4
RELU = mybir.ActivationFunctionType.Relu

G, S, M, H, E, C = 2, 512, 512, 1024, 16, 64
P = 128
PACK = 4
SLOTS = E * C
BANK = 512
PAIR = 2
RUN = 2

MASK_VECTOR_COLUMNS = 640
EVEN_VECTOR_COLUMNS = 512
PASS_COLUMNS = 256
PASS_STEP = 128

HEAD_PIECES = 2
RAW_BUFS = 8
AHEAD = 2

FLOPS = 2 * G * SLOTS * S * M + 2 * E * G * C * M * H


def tile_flaxpositionwisemoelayer_pa_kernel(tc, dispatch_mask, x, wi, out):
    nc = tc.nc
    with ExitStack() as ctx:
        keep = ctx.enter_context(tc.tile_pool(name="keep", bufs=1))
        x_raw_pool = ctx.enter_context(tc.tile_pool(name="x_raw_pool", bufs=HEAD_PIECES + 1))
        x_pool = ctx.enter_context(tc.tile_pool(name="x_pool", bufs=G))
        raw_pool = ctx.enter_context(tc.tile_pool(name="raw_pool", bufs=RAW_BUFS))
        grouped_pool = ctx.enter_context(tc.tile_pool(name="grouped_pool", bufs=AHEAD + 2))
        w_pool = ctx.enter_context(tc.tile_pool(name="w_pool", bufs=3))
        d_grouped_pool = ctx.enter_context(tc.tile_pool(name="d_grouped_pool", bufs=E // PAIR))
        d_pool = ctx.enter_context(tc.tile_pool(name="d_pool", bufs=3))
        result_pool = ctx.enter_context(tc.tile_pool(name="result_pool", bufs=E))
        banks = ctx.enter_context(tc.psum_pool(name="banks", bufs=7))
        pass_psum = ctx.enter_context(tc.psum_pool(name="pass_psum", bufs=1))
        ctx.enter_context(tc.manual_schedule())

        mask_rows = [dispatch_mask[g].rearrange("s e c -> s (e c)") for g in range(G)]
        piece = SLOTS // HEAD_PIECES
        unit_rows = (
            [mask_rows[0][:, h * piece : (h + 1) * piece] for h in range(HEAD_PIECES)]
            + [mask_rows[1]]
            + [wi[e] for e in range(E)]
        )
        MASK1 = HEAD_PIECES
        W0 = HEAD_PIECES + 1
        UNITS = len(unit_rows)

        x_raw, x_grouped, x_codes, x_scales = {}, {}, {}, {}
        raw, grouped, codes, scales = {}, {}, {}, {}
        d_grouped, d_codes, d_scales = {}, {}, {}
        pre, result = {}, {}
        passed = {}

        identity = keep.tile([P, P], BF16, name="identity")
        masks.make_identity(nc, identity[:])

        def load_x(g, pieces):
            width = M // pieces
            for h in range(pieces):
                x_raw[g, h] = x_raw_pool.tile([P, PACK, width], BF16, name="x_raw", tag="x_raw")
                nc.sync.dma_start(
                    out=x_raw[g, h][:],
                    in_=x[g][:, h * width : (h + 1) * width].rearrange("(p j) m -> p j m", j=PACK),
                )

        def load_unit(u):
            width = unit_rows[u].shape[1]
            raw[u] = raw_pool.tile([P, PACK, width], BF16, name="raw", tag="raw")
            nc.sync.dma_start(out=raw[u][:], in_=unit_rows[u].rearrange("(p j) w -> p j w", j=PACK))

        def regroup_x(g, loaded_pieces):
            pieces = HEAD_PIECES
            width = M // pieces
            x_grouped[g] = x_pool.tile(
                [P, M, PACK], BF16, name="x_grouped", tag="x_grouped", align_bytes=64
            )
            q_count = P // pieces
            for h in range(pieces):
                dst = x_grouped[g][:].rearrange("p (t q) j -> p t q j", t=PACK)[
                    :, :, h * q_count : (h + 1) * q_count, :
                ].rearrange("p t (r i) j -> p t r j i", i=RUN)
                if loaded_pieces == pieces:
                    columns = x_raw[g, h][:]
                else:
                    columns = x_raw[g, 0][:, :, h * width : (h + 1) * width]
                src = columns.rearrange("p j (r i t) -> p t r j i", i=RUN, t=PACK)
                nc.vector.tensor_copy(out=dst, in_=src)

        def quantise_x(g):
            x_codes[g] = keep.tile([P, M], U32, name="x_codes%d" % g, align_bytes=64)
            x_scales[g] = keep.tile([P, M], U8, name="x_scales%d" % g, align_bytes=64)
            nc.vector.quantize_mx(
                out=x_codes[g][:].bitcast(FP8X4),
                scales=x_scales[g][:],
                in_=x_grouped[g][:].rearrange("p w j -> p (w j)"),
            )

        def is_passed(u):
            return u >= W0 and (u - W0) % 2 == 1

        def pass_through(u):
            passed[u] = pass_psum.tile([P, PASS_COLUMNS, PACK], BF16, name="passed", tag="passed")
            for first in range(0, PASS_COLUMNS, PASS_STEP):
                start = H - PASS_COLUMNS + first
                nc.tensor.matmul(
                    out=passed[u][:, first : first + PASS_STEP, :],
                    lhsT=identity[:],
                    rhs=raw[u][:, :, start : start + PASS_STEP].rearrange("p j c -> p c j"),
                    start=True,
                    stop=True,
                )

        def regroup_unit(u):
            width = unit_rows[u].shape[1]
            if is_passed(u):
                border = width - PASS_COLUMNS
            else:
                share = MASK_VECTOR_COLUMNS if u < W0 else EVEN_VECTOR_COLUMNS
                border = share * width // H
            grouped[u] = grouped_pool.tile(
                [P, width, PACK], BF16, name="grouped", tag="grouped", align_bytes=64
            )
            dst = grouped[u][:].rearrange("p (r i) j -> p r j i", i=RUN)
            src = raw[u][:].rearrange("p j (r i) -> p r j i", i=RUN)
            runs = border // RUN
            nc.vector.tensor_copy(out=dst[:, :runs], in_=src[:, :runs])
            if is_passed(u):
                nc.scalar.copy(
                    out=grouped[u][:, border:, :].rearrange("p c j -> p (c j)"),
                    in_=passed[u][:].rearrange("p c j -> p (c j)"),
                )
            else:
                nc.scalar.copy(out=dst[:, runs:], in_=src[:, runs:])
            if u + RAW_BUFS < UNITS:
                load_unit(u + RAW_BUFS)

        def quantise_unit(u, pieces=1, after_piece=None):
            width = unit_rows[u].shape[1]
            if u < W0:
                codes[u] = keep.tile([P, width], U32, name="mask_codes%d" % u, align_bytes=64)
                scales[u] = keep.tile([P, width], U8, name="mask_scales%d" % u, align_bytes=64)
            else:
                codes[u] = w_pool.tile([P, H], U32, name="w_codes", tag="w_codes", align_bytes=64)
                scales[u] = w_pool.tile([P, H], U8, name="w_scales", tag="w_scales", align_bytes=64)
            for first in range(0, width, width // pieces):
                cols = slice(first, first + width // pieces)
                nc.vector.quantize_mx(
                    out=codes[u][:, cols].bitcast(FP8X4),
                    scales=scales[u][:, cols],
                    in_=grouped[u][:, cols, :].rearrange("p w j -> p (w j)"),
                )
                if after_piece is not None:
                    after_piece(first)

        def dispatch(pair, g):
            bank = banks.tile([P, PACK, PAIR * C], F32, name="bank", tag="bank")
            first = pair * PAIR * C
            u = first // piece if g == 0 else MASK1
            if g == 0:
                first = first % piece
            slots = slice(first, first + PAIR * C)
            for t in range(PACK):
                m_slice = slice(t * P, (t + 1) * P)
                nc.tensor.matmul_mx(
                    out=bank[:, t, :],
                    lhsT=x_codes[g][:, m_slice].bitcast(FP8X4),
                    lhsT_scale=x_scales[g][:, m_slice],
                    rhs=codes[u][:, slots].bitcast(FP8X4),
                    rhs_scale=scales[u][:, slots],
                    start=True,
                    stop=True,
                )
            if g == 0:
                d_grouped[pair] = d_grouped_pool.tile(
                    [P, PAIR, G, C, PACK], BF16, name="d_grouped", tag="d_grouped", align_bytes=64
                )
            nc.scalar.copy(
                out=d_grouped[pair][:, :, g, :, :],
                in_=bank[:].rearrange("p t (e c) -> p e c t", e=PAIR),
            )

        def quantise_dispatched(pair):
            d_codes[pair] = d_pool.tile(
                [P, PAIR * G * C], U32, name="d_codes", tag="d_codes", align_bytes=64
            )
            d_scales[pair] = d_pool.tile(
                [P, PAIR * G * C], U8, name="d_scales", tag="d_scales", align_bytes=64
            )
            nc.vector.quantize_mx(
                out=d_codes[pair][:].bitcast(FP8X4),
                scales=d_scales[pair][:],
                in_=d_grouped[pair][:].rearrange("p e g c t -> p (e g c t)"),
            )

        def project_columns(e, first, width):
            pair = e // PAIR
            rows = slice((e % PAIR) * G * C, (e % PAIR + 1) * G * C)
            h_cols = slice(first, first + width)
            pre[e, first] = banks.tile([P, width], F32, name="bank", tag="bank")
            nc.tensor.matmul_mx(
                out=pre[e, first][:],
                lhsT=d_codes[pair][:, rows].bitcast(FP8X4),
                lhsT_scale=d_scales[pair][:, rows],
                rhs=codes[W0 + e][:, h_cols].bitcast(FP8X4),
                rhs_scale=scales[W0 + e][:, h_cols],
                start=True,
                stop=True,
            )

        def project(e):
            for first in range(0, H, BANK):
                project_columns(e, first, BANK)

        def relu_columns(e, first, width, on_vector=False):
            h_cols = slice(first, first + width)
            if on_vector:
                nc.vector.tensor_scalar_max(
                    out=result[e][:, h_cols], in0=pre[e, first][:], scalar1=0.0
                )
            else:
                nc.scalar.activation(out=result[e][:, h_cols], in_=pre[e, first][:], func=RELU)

        def relu(e):
            result[e] = result_pool.tile([P, H], F32, name="result", tag="result")
            for first in range(0, H, BANK):
                relu_columns(e, first, BANK)

        def store_columns(e, first, width):
            h_cols = slice(first, first + width)
            nc.sync.dma_start(
                out=out[e].rearrange("g c h -> (g c) h")[:, h_cols], in_=result[e][:, h_cols]
            )

        load_x(0, HEAD_PIECES)
        for u in range(MASK1):
            load_unit(u)
        load_x(1, 1)
        for u in range(MASK1, RAW_BUFS):
            load_unit(u)

        warm = keep.tile([P, 1], F32, name="warm")
        nc.vector.memset(warm[:], 0.0)
        nc.scalar.activation(out=warm[:], in_=warm[:], func=RELU)

        pairs_a_piece = E // PAIR // HEAD_PIECES
        regroup_x(0, HEAD_PIECES)
        regroup_unit(0)
        quantise_x(0)
        quantise_unit(0)
        regroup_unit(1)
        regroup_x(1, 1)
        for pair in range(pairs_a_piece):
            dispatch(pair, 0)
        quantise_unit(1)
        regroup_unit(MASK1)
        quantise_x(1)
        for pair in range(pairs_a_piece, E // PAIR):
            dispatch(pair, 0)
        regroup_unit(W0)
        quantise_unit(MASK1)
        dispatch(0, 1)
        pass_through(W0 + 1)
        regroup_unit(W0 + 1)

        for e in range(E - 1):
            if e + AHEAD < E:
                regroup_unit(W0 + e + AHEAD)
            if e % PAIR == 0:
                if e + PAIR < E:
                    dispatch(e // PAIR + 1, 1)
                quantise_dispatched(e // PAIR)
            quantise_unit(W0 + e)
            if e + AHEAD + 1 < E and is_passed(W0 + e + AHEAD + 1):
                pass_through(W0 + e + AHEAD + 1)
            project(e)
            if e >= 1:
                relu(e - 1)

        last = E - 1
        result[last] = result_pool.tile([P, H], F32, name="result", tag="result")

        def project_piece(first):
            if first == 0:
                project_columns(last, 0, BANK)
                relu(last - 1)
            else:
                project_columns(last, BANK, BANK // 2)
                project_columns(last, BANK + BANK // 2, BANK // 2)

        quantise_unit(W0 + last, pieces=H // BANK, after_piece=project_piece)
        relu_columns(last, 0, BANK)
        relu_columns(last, BANK, BANK // 2, on_vector=True)
        relu_columns(last, BANK + BANK // 2, BANK // 2)

        for e in range(E - 1):
            store_columns(e, 0, H)
        for first in range(0, H, BANK):
            store_columns(last, first, BANK)
